import numpy as np
import ml_dtypes


def mxq(x, axis, fmt="e4m3"):
    dtype, down = {"e4m3": (ml_dtypes.float8_e4m3fn, 7), "e5m2": (ml_dtypes.float8_e5m2, 14)}[fmt]
    v = np.moveaxis(np.asarray(x, np.float32).astype(ml_dtypes.bfloat16).astype(np.float64), axis, -1)
    blocks = v.reshape(v.shape[:-1] + (-1, 32))
    amax = np.abs(blocks).max(-1, keepdims=True)
    byte = np.maximum(np.where(amax > 0, np.frexp(amax)[1] - 1 + 127, 0) - down, 1)
    scale = np.exp2(byte - 127.0)
    codes = (blocks / scale).astype(np.float32).astype(dtype).astype(np.float64)
    return np.moveaxis((codes * scale).reshape(v.shape), -1, axis)


WIDE = False


def mx_kscale(k):
    if not WIDE:
        return np.ones(k)
    levels = np.array([10, -10, 5, -5, 0])
    if k % 512:
        return np.exp2(np.random.permutation(np.resize(levels, k // 32))).repeat(32)
    a = np.empty((k // 512, 16))
    for p in range(k // 512):
        a[p, :8] = np.random.permutation(np.resize(levels, 8))
        for g in range(8):
            far = levels[np.abs(levels - a[p, g]) >= 10]
            a[p, g + 8] = far[np.random.randint(len(far))]
    return np.exp2(a.ravel()).repeat(32)


BF16 = ml_dtypes.bfloat16


def bf(x):
    return np.asarray(x, np.float32).astype(BF16)


def f64(x):
    return np.asarray(x).astype(np.float64)


B, X, N, OS = 2048, 512, 2304, 256
H = N - OS


def setup_inputs():
    s, t = mx_kscale(X), mx_kscale(H)
    std0 = np.sqrt(2.0 / X)
    std1 = np.sqrt(2.0 / (X + H))
    row_scale = np.concatenate([std0 * t, np.full(OS, std1)])
    bias_scale = np.concatenate([t, np.ones(OS)])
    return {"x": bf(np.random.standard_normal((B, X)) * s),
            "w0": bf(np.random.standard_normal((N, X)) * row_scale[:, None] / s),
            "w1": bf(np.random.standard_normal((OS, H)) * std1 / t),
            "biases": bf(np.random.random(N) * bias_scale)}


def reference(x, w0, w1, biases):
    n = w0.shape[0]
    os_ = w1.shape[0]
    z = (mxq(f64(x), 1, "e4m3") @ mxq(f64(w0), 1, "e4m3").T) + f64(biases)
    h = np.maximum(z[:, : n - os_], 0.0)
    return z[:, n - os_:] + (mxq(h, 1, "e4m3") @ mxq(f64(w1), 1, "e4m3").T)

@@ -1,0 +1,281 @@
+import concourse.mybir as mybir
+from concourse.masks import make_identity
+
+BF16 = mybir.dt.bfloat16
+F32 = mybir.dt.float32
+U32 = mybir.dt.uint32
+U8 = mybir.dt.uint8
+FP8X4 = mybir.dt.float8_e4m3fn_x4
+RELU = mybir.ActivationFunctionType.Relu
+ADD = mybir.AluOpType.add
+
+P = 128
+PACK = 4
+K_PASS = P * PACK
+HALF = 2
+
+BATCH = 2048
+X_DIM = 512
+HIDDEN = 2048
+OUT_NODES = 256
+
+CHUNK = 512
+CHUNKS = BATCH // CHUNK
+GROUPS = HIDDEN // K_PASS
+
+STEPS = CHUNKS * GROUPS
+LAG = 2
+PIECES = 2
+
+AT_ONCE = 2
+PER_STEP = 2
+VECTOR_EVERY = 3
+
+FLOPS = 2 * BATCH * X_DIM * (HIDDEN + OUT_NODES) + 2 * BATCH * HIDDEN * OUT_NODES
+
+
+def tile_spn_kernel(tc, x, w0, w1, biases, out):
+    nc = tc.nc
+    with (
+        tc.tile_pool(name="const", bufs=1) as const,
+        tc.tile_pool(name="rows", bufs=1) as rows_pool,
+        tc.tile_pool(name="quantised", bufs=1) as quantised,
+        tc.tile_pool(name="grouped", bufs=3) as grouped_pool,
+        tc.tile_pool(name="planes", bufs=3) as planes_pool,
+        tc.tile_pool(name="hidden", bufs=2) as hidden_pool,
+        tc.tile_pool(name="result", bufs=4) as result_pool,
+        tc.psum_pool(name="banks", bufs=4) as banks,
+        tc.psum_pool(name="sums", bufs=1) as sums,
+        tc.manual_schedule(),
+    ):
+        hidden_bias = const.tile([P, GROUPS, PACK], BF16)
+        nc.scalar.dma_start(
+            out=hidden_bias[:],
+            in_=biases[0:HIDDEN].rearrange("(g p t) -> p g t", p=P, t=PACK),
+        )
+        identity = const.tile([P, P], F32)
+        make_identity(nc, identity[:])
+        warm_up = const.tile([P, 1], F32)
+        nc.vector.memset(warm_up[:], 0.0)
+        nc.scalar.activation(out=warm_up[:], in_=warm_up[:], func=RELU)
+
+        x_codes = quantised.tile([P, BATCH], U32, align_bytes=64)
+        x_scales = quantised.tile([P, BATCH], U8, align_bytes=64)
+        w0_codes = quantised.tile([P, HIDDEN], U32, align_bytes=64)
+        w0_scales = quantised.tile([P, HIDDEN], U8, align_bytes=64)
+        w0_out_codes = quantised.tile([P, OUT_NODES], U32, align_bytes=64)
+        w0_out_scales = quantised.tile([P, OUT_NODES], U8, align_bytes=64)
+        w1_codes = quantised.tile([P, GROUPS * OUT_NODES], U32, align_bytes=64)
+        w1_scales = quantised.tile([P, GROUPS * OUT_NODES], U8, align_bytes=64)
+
+        def halves_alternating(rows, g):
+            words = rows.bitcast(F32)
+            return [words[:, HALF * P * g + u : HALF * P * (g + 1) : HALF] for u in range(HALF)]
+
+        def block_of_512_rows(source, first, name, codes, scales):
+            by_partition = source[first : first + K_PASS, :].rearrange("(p j) k -> p j k", j=PACK)
+            row_tiles = []
+            for j in range(0, PACK, 2):
+                rows = rows_pool.tile([P, 2, X_DIM], BF16, name="%s_%d" % (name, j))
+                nc.sync.dma_start(out=rows[:], in_=by_partition[:, j : j + 2, :])
+                row_tiles += [halves_alternating(rows[:, r, :], 0) for r in range(2)]
+            columns = slice(first, first + K_PASS)
+            return row_tiles, codes[:, columns], scales[:, columns]
+
+        def x_chunk(c):
+            return block_of_512_rows(x, c * CHUNK, "x_rows%d" % c, x_codes, x_scales)
+
+        def w0_group(g):
+            return block_of_512_rows(w0, g * K_PASS, "w0_rows%d" % g, w0_codes, w0_scales)
+
+        operands = [x_chunk(0)] + [w0_group(g) for g in range(GROUPS - 1)]
+
+        w0_out_rows = rows_pool.tile([P, OUT_NODES // P, X_DIM], BF16)
+        nc.sync.dma_start(
+            out=w0_out_rows[:],
+            in_=w0[HIDDEN : HIDDEN + OUT_NODES, :].rearrange("(a p) k -> p a k", p=P),
+        )
+        operands.append(
+            (
+                [halves_alternating(w0_out_rows[:, a, :], 0) for a in range(OUT_NODES // P)],
+                w0_out_codes[:],
+                w0_out_scales[:],
+            )
+        )
+        w1_rows = rows_pool.tile([P, OUT_NODES // P, HIDDEN], BF16)
+        nc.sync.dma_start(out=w1_rows[:], in_=w1.rearrange("(a p) k -> p a k", p=P))
+
+        def w1_two_groups(first_g):
+            columns = slice(first_g * OUT_NODES, (first_g + 2) * OUT_NODES)
+            row_tiles = [
+                halves_alternating(w1_rows[:, a, :], g)
+                for g in range(first_g, first_g + 2)
+                for a in range(OUT_NODES // P)
+            ]
+            return row_tiles, w1_codes[:, columns], w1_scales[:, columns]
+
+        operands += [w1_two_groups(0), w0_group(GROUPS - 1), x_chunk(1), w1_two_groups(2)]
+        operands += [x_chunk(c) for c in range(2, CHUNKS)]
+
+        out_bias_bf = const.tile([P, OUT_NODES], BF16)
+        nc.sync.dma_start(
+            out=out_bias_bf[:], in_=biases[HIDDEN : HIDDEN + OUT_NODES].partition_broadcast(P)
+        )
+        out_bias = const.tile([P, OUT_NODES], F32)
+        nc.gpsimd.tensor_copy(out=out_bias[:], in_=out_bias_bf[:])
+
+        grouped_of = {}
+
+        def transpose_operand(i):
+            row_tiles = operands[i][0]
+            grouped = grouped_pool.tile(
+                [P, PACK * K_PASS], BF16, align_bytes=64, name="grouped"
+            )
+            grouped_of[i] = grouped
+            grouped_words = grouped[:].bitcast(F32)
+            for first in range(0, len(row_tiles), 2):
+                bank = banks.tile([P, CHUNK], F32, name="bank")
+                for r in range(2):
+                    for u in range(HALF):
+                        quarter = HALF * r + u
+                        nc.tensor.transpose(
+                            bank[:, P * quarter : P * (quarter + 1)],
+                            row_tiles[first + r][u],
+                            identity[:],
+                        )
+                bank_number = i * 2 + first // 2
+                if bank_number % VECTOR_EVERY == 0:
+                    copy = nc.vector.tensor_copy
+                else:
+                    copy = nc.scalar.copy
+                copy(
+                    out=grouped_words[:, HALF * P * first : HALF * P * (first + 2)].rearrange(
+                        "p (r b u) -> p r b u", r=2, u=HALF
+                    ),
+                    in_=bank[:].rearrange("p (r u b) -> p r b u", r=2, u=HALF),
+                )
+
+        def quantise_operand(i):
+            row_tiles, codes, scales = operands[i]
+            nc.vector.quantize_mx(
+                out=codes.bitcast(FP8X4),
+                scales=scales,
+                in_=grouped_of[i][:, 0 : PACK * P * len(row_tiles)],
+            )
+
+        def prepare(i):
+            if i < len(operands):
+                transpose_operand(i)
+            if AT_ONCE < i <= len(operands):
+                quantise_operand(i - 1)
+
+        def first_stage(c, g):
+            planes = planes_pool.tile([P, PACK, CHUNK], BF16, name="planes")
+            for t in range(PACK):
+                nodes = slice(g * K_PASS + t * P, g * K_PASS + (t + 1) * P)
+                batch = slice(c * CHUNK, (c + 1) * CHUNK)
+                bank = banks.tile([P, CHUNK], F32, name="bank")
+                nc.tensor.matmul_mx(
+                    out=bank[:],
+                    lhsT=w0_codes[:, nodes].bitcast(FP8X4),
+                    lhsT_scale=w0_scales[:, nodes],
+                    rhs=x_codes[:, batch].bitcast(FP8X4),
+                    rhs_scale=x_scales[:, batch],
+                    start=True,
+                    stop=True,
+                )
+                nc.scalar.activation(
+                    out=planes[:, t, :],
+                    in_=bank[:],
+                    func=RELU,
+                    bias=hidden_bias[:, g, t : t + 1],
+                    scale=1.0,
+                )
+            return planes
+
+        def regroup_and_quantise(planes, codes, scales):
+            h_grouped = hidden_pool.tile([P, PACK * CHUNK], BF16, align_bytes=64, name="h_grouped")
+            width = CHUNK // PIECES
+            for piece in range(PIECES):
+                batch = slice(piece * width, (piece + 1) * width)
+                nc.vector.tensor_copy(
+                    out=h_grouped[:, PACK * piece * width : PACK * (piece + 1) * width].rearrange(
+                        "p (c i t) -> p c t i", i=4, t=PACK
+                    ),
+                    in_=planes[:, :, batch].rearrange("p t (c i) -> p c t i", i=4),
+                )
+            for piece in range(PIECES):
+                batch = slice(piece * width, (piece + 1) * width)
+                nc.vector.quantize_mx(
+                    out=codes[:, batch].bitcast(FP8X4),
+                    scales=scales[:, batch],
+                    in_=h_grouped[:, PACK * piece * width : PACK * (piece + 1) * width],
+                )
+
+        def second_stage(c, g, h_codes, h_scales, accs):
+            weights = slice(g * OUT_NODES, (g + 1) * OUT_NODES)
+            for j in range(PACK):
+                if g == 0:
+                    batch = slice(c * CHUNK + j * P, c * CHUNK + (j + 1) * P)
+                    nc.tensor.matmul_mx(
+                        out=accs[j][:],
+                        lhsT=x_codes[:, batch].bitcast(FP8X4),
+                        lhsT_scale=x_scales[:, batch],
+                        rhs=w0_out_codes[:].bitcast(FP8X4),
+                        rhs_scale=w0_out_scales[:],
+                        start=True,
+                        stop=False,
+                    )
+                batch = slice(g * CHUNK + j * P, g * CHUNK + (j + 1) * P)
+                nc.tensor.matmul_mx(
+                    out=accs[j][:],
+                    lhsT=h_codes[:, batch].bitcast(FP8X4),
+                    lhsT_scale=h_scales[:, batch],
+                    rhs=w1_codes[:, weights].bitcast(FP8X4),
+                    rhs_scale=w1_scales[:, weights],
+                    start=False,
+                    stop=(g == GROUPS - 1),
+                )
+
+        def finish(c, accs):
+            rows_of_out = out[c * CHUNK : (c + 1) * CHUNK, :].rearrange("(p j) o -> p j o", j=PACK)
+            for j in range(PACK):
+                result = result_pool.tile([P, OUT_NODES], F32, name="result")
+                nc.vector.tensor_tensor(out=result[:], in0=accs[j][:], in1=out_bias[:], op=ADD)
+                nc.sync.dma_start(out=rows_of_out[:, j, :], in_=result[:])
+
+        for i in range(AT_ONCE):
+            transpose_operand(i)
+            quantise_operand(i)
+        prepare(AT_ONCE)
+
+        h_codes_of = {}
+        h_scales_of = {}
+        accs_of = {}
+        for step in range(STEPS + LAG):
+            if step < STEPS:
+                c, g = divmod(step, GROUPS)
+                if g == 0:
+                    h_codes_of[c] = hidden_pool.tile(
+                        [P, GROUPS * CHUNK], U32, align_bytes=64, name="h_codes"
+                    )
+                    h_scales_of[c] = hidden_pool.tile(
+                        [P, GROUPS * CHUNK], U8, align_bytes=64, name="h_scales"
+                    )
+                planes = first_stage(c, g)
+            if step >= LAG:
+                late_c, late_g = divmod(step - LAG, GROUPS)
+                if late_g == 0:
+                    accs_of[late_c] = [
+                        sums.tile([P, OUT_NODES], F32, name="acc%d" % j) for j in range(PACK)
+                    ]
+                second_stage(
+                    late_c, late_g, h_codes_of[late_c], h_scales_of[late_c], accs_of[late_c]
+                )
+                if late_g == GROUPS - 1:
+                    finish(late_c, accs_of[late_c])
+            for i in range(PER_STEP):
+                prepare(AT_ONCE + 1 + PER_STEP * step + i)
+            if step < STEPS:
+                columns = slice(g * CHUNK, (g + 1) * CHUNK)
+                regroup_and_quantise(planes, h_codes_of[c][:, columns], h_scales_of[c][:, columns])

@@ -21,14 +21,14 @@ OUT_NODES = 256
 
 CHUNK = 512
 CHUNKS = BATCH // CHUNK
+TILES = CHUNK // P
 GROUPS = HIDDEN // K_PASS
-
 STEPS = CHUNKS * GROUPS
-LAG = 2
-PIECES = 2
 
-AT_ONCE = 2
-PER_STEP = 2
+PIECE = 256
+
+FIRST_PIECES = 6
+LATE_TILES = [(), (0, 1), (2,), (3,)]
 VECTOR_EVERY = 3
 
 FLOPS = 2 * BATCH * X_DIM * (HIDDEN + OUT_NODES) + 2 * BATCH * HIDDEN * OUT_NODES
@@ -40,12 +40,12 @@ def tile_spn_kernel(tc, x, w0, w1, biases, out):
         tc.tile_pool(name="const", bufs=1) as const,
         tc.tile_pool(name="rows", bufs=1) as rows_pool,
         tc.tile_pool(name="quantised", bufs=1) as quantised,
-        tc.tile_pool(name="grouped", bufs=3) as grouped_pool,
+        tc.tile_pool(name="grouped", bufs=4) as grouped_pool,
         tc.tile_pool(name="planes", bufs=3) as planes_pool,
         tc.tile_pool(name="hidden", bufs=2) as hidden_pool,
         tc.tile_pool(name="result", bufs=4) as result_pool,
-        tc.psum_pool(name="banks", bufs=4) as banks,
-        tc.psum_pool(name="sums", bufs=1) as sums,
+        tc.psum_pool(name="banks", bufs=6) as banks,
+        tc.psum_pool(name="sums", bufs=2) as sums,
         tc.manual_schedule(),
     ):
         hidden_bias = const.tile([P, GROUPS, PACK], BF16)
@@ -61,61 +61,74 @@ def tile_spn_kernel(tc, x, w0, w1, biases, out):
 
         x_codes = quantised.tile([P, BATCH], U32, align_bytes=64)
         x_scales = quantised.tile([P, BATCH], U8, align_bytes=64)
-        w0_codes = quantised.tile([P, HIDDEN], U32, align_bytes=64)
-        w0_scales = quantised.tile([P, HIDDEN], U8, align_bytes=64)
-        w0_out_codes = quantised.tile([P, OUT_NODES], U32, align_bytes=64)
-        w0_out_scales = quantised.tile([P, OUT_NODES], U8, align_bytes=64)
+        w0_codes = quantised.tile([P, HIDDEN + OUT_NODES], U32, align_bytes=64)
+        w0_scales = quantised.tile([P, HIDDEN + OUT_NODES], U8, align_bytes=64)
         w1_codes = quantised.tile([P, GROUPS * OUT_NODES], U32, align_bytes=64)
         w1_scales = quantised.tile([P, GROUPS * OUT_NODES], U8, align_bytes=64)
 
-        def halves_alternating(rows, g):
+        pieces = []
+
+        def row_tile(rows, g):
             words = rows.bitcast(F32)
             return [words[:, HALF * P * g + u : HALF * P * (g + 1) : HALF] for u in range(HALF)]
 
-        def block_of_512_rows(source, first, name, codes, scales):
+        def two_pieces_of_512_rows(source, first, name, codes, scales):
             by_partition = source[first : first + K_PASS, :].rearrange("(p j) k -> p j k", j=PACK)
-            row_tiles = []
+            halves = []
             for j in range(0, PACK, 2):
-                rows = rows_pool.tile([P, 2, X_DIM], BF16, name="%s_%d" % (name, j))
-                nc.sync.dma_start(out=rows[:], in_=by_partition[:, j : j + 2, :])
-                row_tiles += [halves_alternating(rows[:, r, :], 0) for r in range(2)]
-            columns = slice(first, first + K_PASS)
-            return row_tiles, codes[:, columns], scales[:, columns]
+                columns = slice(first + P * j, first + P * j + PIECE)
+
+                def load(j=j, columns=columns):
+                    rows = rows_pool.tile([P, 2, X_DIM], BF16, name="%s_%d" % (name, j))
+                    nc.sync.dma_start(out=rows[:], in_=by_partition[:, j : j + 2, :])
+                    row_tiles = [row_tile(rows[:, r, :], 0) for r in range(2)]
+                    pieces.append((row_tiles, codes[:, columns], scales[:, columns]))
+
+                halves.append(load)
+            return halves
 
         def x_chunk(c):
-            return block_of_512_rows(x, c * CHUNK, "x_rows%d" % c, x_codes, x_scales)
+            return two_pieces_of_512_rows(x, c * CHUNK, "x_rows%d" % c, x_codes, x_scales)
 
         def w0_group(g):
-            return block_of_512_rows(w0, g * K_PASS, "w0_rows%d" % g, w0_codes, w0_scales)
+            return two_pieces_of_512_rows(w0, g * K_PASS, "w0_rows%d" % g, w0_codes, w0_scales)
 
-        operands = [x_chunk(0)] + [w0_group(g) for g in range(GROUPS - 1)]
+        for halves in zip(x_chunk(0), w0_group(0)):
+            for load in halves:
+                load()
+        for g in range(1, GROUPS):
+            for load in w0_group(g):
+                load()
+        for load in x_chunk(1):
+            load()
 
         w0_out_rows = rows_pool.tile([P, OUT_NODES // P, X_DIM], BF16)
         nc.sync.dma_start(
             out=w0_out_rows[:],
             in_=w0[HIDDEN : HIDDEN + OUT_NODES, :].rearrange("(a p) k -> p a k", p=P),
         )
-        operands.append(
+        out_columns = slice(HIDDEN, HIDDEN + OUT_NODES)
+        pieces.append(
             (
-                [halves_alternating(w0_out_rows[:, a, :], 0) for a in range(OUT_NODES // P)],
-                w0_out_codes[:],
-                w0_out_scales[:],
+                [row_tile(w0_out_rows[:, a, :], 0) for a in range(OUT_NODES // P)],
+                w0_codes[:, out_columns],
+                w0_scales[:, out_columns],
             )
         )
         w1_rows = rows_pool.tile([P, OUT_NODES // P, HIDDEN], BF16)
         nc.sync.dma_start(out=w1_rows[:], in_=w1.rearrange("(a p) k -> p a k", p=P))
-
-        def w1_two_groups(first_g):
-            columns = slice(first_g * OUT_NODES, (first_g + 2) * OUT_NODES)
-            row_tiles = [
-                halves_alternating(w1_rows[:, a, :], g)
-                for g in range(first_g, first_g + 2)
-                for a in range(OUT_NODES // P)
-            ]
-            return row_tiles, w1_codes[:, columns], w1_scales[:, columns]
-
-        operands += [w1_two_groups(0), w0_group(GROUPS - 1), x_chunk(1), w1_two_groups(2)]
-        operands += [x_chunk(c) for c in range(2, CHUNKS)]
+        for g in range(GROUPS):
+            columns = slice(g * OUT_NODES, (g + 1) * OUT_NODES)
+            pieces.append(
+                (
+                    [row_tile(w1_rows[:, a, :], g) for a in range(OUT_NODES // P)],
+                    w1_codes[:, columns],
+                    w1_scales[:, columns],
+                )
+            )
+        for c in range(2, CHUNKS):
+            for load in x_chunk(c):
+                load()
 
         out_bias_bf = const.tile([P, OUT_NODES], BF16)
         nc.sync.dma_start(
@@ -126,54 +139,41 @@ def tile_spn_kernel(tc, x, w0, w1, biases, out):
 
         grouped_of = {}
 
-        def transpose_operand(i):
-            row_tiles = operands[i][0]
-            grouped = grouped_pool.tile(
-                [P, PACK * K_PASS], BF16, align_bytes=64, name="grouped"
-            )
+        def transpose_piece(i):
+            bank = banks.tile([P, CHUNK], F32, name="bank")
+            for r in range(2):
+                for u in range(HALF):
+                    quarter = HALF * r + u
+                    nc.tensor.transpose(
+                        bank[:, P * quarter : P * (quarter + 1)],
+                        pieces[i][0][r][u],
+                        identity[:],
+                    )
+            grouped = grouped_pool.tile([P, PACK * PIECE], BF16, align_bytes=64, name="grouped")
             grouped_of[i] = grouped
-            grouped_words = grouped[:].bitcast(F32)
-            for first in range(0, len(row_tiles), 2):
-                bank = banks.tile([P, CHUNK], F32, name="bank")
-                for r in range(2):
-                    for u in range(HALF):
-                        quarter = HALF * r + u
-                        nc.tensor.transpose(
-                            bank[:, P * quarter : P * (quarter + 1)],
-                            row_tiles[first + r][u],
-                            identity[:],
-                        )
-                bank_number = i * 2 + first // 2
-                if bank_number % VECTOR_EVERY == 0:
-                    copy = nc.vector.tensor_copy
-                else:
-                    copy = nc.scalar.copy
-                copy(
-                    out=grouped_words[:, HALF * P * first : HALF * P * (first + 2)].rearrange(
-                        "p (r b u) -> p r b u", r=2, u=HALF
-                    ),
-                    in_=bank[:].rearrange("p (r u b) -> p r b u", r=2, u=HALF),
-                )
-
-        def quantise_operand(i):
-            row_tiles, codes, scales = operands[i]
-            nc.vector.quantize_mx(
-                out=codes.bitcast(FP8X4),
-                scales=scales,
-                in_=grouped_of[i][:, 0 : PACK * P * len(row_tiles)],
+            copy = nc.vector.tensor_copy if i % VECTOR_EVERY == 0 else nc.scalar.copy
+            copy(
+                out=grouped[:].bitcast(F32).rearrange("p (r b u) -> p r b u", r=2, u=HALF),
+                in_=bank[:].rearrange("p (r u b) -> p r b u", r=2, u=HALF),
             )
 
-        def prepare(i):
-            if i < len(operands):
-                transpose_operand(i)
-            if AT_ONCE < i <= len(operands):
-                quantise_operand(i - 1)
+        def quantise_piece(i):
+            nc.vector.quantize_mx(
+                out=pieces[i][1].bitcast(FP8X4), scales=pieces[i][2], in_=grouped_of[i][:]
+            )
 
-        def first_stage(c, g):
+        h_codes_of = {}
+        h_scales_of = {}
+        planes_of = {}
+        accs_of = {}
+
+        def first_stage(step):
+            c, g = divmod(step, GROUPS)
             planes = planes_pool.tile([P, PACK, CHUNK], BF16, name="planes")
+            planes_of[step] = planes
+            batch = slice(c * CHUNK, (c + 1) * CHUNK)
             for t in range(PACK):
                 nodes = slice(g * K_PASS + t * P, g * K_PASS + (t + 1) * P)
-                batch = slice(c * CHUNK, (c + 1) * CHUNK)
                 bank = banks.tile([P, CHUNK], F32, name="bank")
                 nc.tensor.matmul_mx(
                     out=bank[:],
@@ -191,91 +191,108 @@ def tile_spn_kernel(tc, x, w0, w1, biases, out):
                     bias=hidden_bias[:, g, t : t + 1],
                     scale=1.0,
                 )
-            return planes
 
-        def regroup_and_quantise(planes, codes, scales):
+        def regroup_and_quantise(step, parts):
+            c, g = divmod(step, GROUPS)
+            if g == 0:
+                h_codes_of[c] = hidden_pool.tile(
+                    [P, GROUPS * CHUNK], U32, align_bytes=64, name="h_codes"
+                )
+                h_scales_of[c] = hidden_pool.tile(
+                    [P, GROUPS * CHUNK], U8, align_bytes=64, name="h_scales"
+                )
+            planes = planes_of.pop(step)
             h_grouped = hidden_pool.tile([P, PACK * CHUNK], BF16, align_bytes=64, name="h_grouped")
-            width = CHUNK // PIECES
-            for piece in range(PIECES):
-                batch = slice(piece * width, (piece + 1) * width)
-                nc.vector.tensor_copy(
-                    out=h_grouped[:, PACK * piece * width : PACK * (piece + 1) * width].rearrange(
-                        "p (c i t) -> p c t i", i=4, t=PACK
-                    ),
-                    in_=planes[:, :, batch].rearrange("p t (c i) -> p c t i", i=4),
-                )
-            for piece in range(PIECES):
-                batch = slice(piece * width, (piece + 1) * width)
-                nc.vector.quantize_mx(
-                    out=codes[:, batch].bitcast(FP8X4),
-                    scales=scales[:, batch],
-                    in_=h_grouped[:, PACK * piece * width : PACK * (piece + 1) * width],
-                )
+            width = CHUNK // parts
+            for part in range(parts + 1):
+                if part < parts:
+                    batch = slice(part * width, (part + 1) * width)
+                    nc.vector.tensor_copy(
+                        out=h_grouped[:, PACK * part * width : PACK * (part + 1) * width].rearrange(
+                            "p (c i t) -> p c t i", i=4, t=PACK
+                        ),
+                        in_=planes[:, :, batch].rearrange("p t (c i) -> p c t i", i=4),
+                    )
+                if part > 0:
+                    first = (part - 1) * width
+                    columns = slice(g * CHUNK + first, g * CHUNK + first + width)
+                    nc.vector.quantize_mx(
+                        out=h_codes_of[c][:, columns].bitcast(FP8X4),
+                        scales=h_scales_of[c][:, columns],
+                        in_=h_grouped[:, PACK * first : PACK * (first + width)],
+                    )
 
-        def second_stage(c, g, h_codes, h_scales, accs):
+        def output_pass(c, j, acc):
+            batch = slice(c * CHUNK + j * P, c * CHUNK + (j + 1) * P)
+            nc.tensor.matmul_mx(
+                out=acc[:, 0:OUT_NODES],
+                lhsT=x_codes[:, batch].bitcast(FP8X4),
+                lhsT_scale=x_scales[:, batch],
+                rhs=w0_codes[:, out_columns].bitcast(FP8X4),
+                rhs_scale=w0_scales[:, out_columns],
+                start=True,
+                stop=False,
+            )
+
+        def hidden_pass(c, j, g, acc):
+            batch = slice(g * CHUNK + j * P, g * CHUNK + (j + 1) * P)
             weights = slice(g * OUT_NODES, (g + 1) * OUT_NODES)
-            for j in range(PACK):
-                if g == 0:
-                    batch = slice(c * CHUNK + j * P, c * CHUNK + (j + 1) * P)
-                    nc.tensor.matmul_mx(
-                        out=accs[j][:],
-                        lhsT=x_codes[:, batch].bitcast(FP8X4),
-                        lhsT_scale=x_scales[:, batch],
-                        rhs=w0_out_codes[:].bitcast(FP8X4),
-                        rhs_scale=w0_out_scales[:],
-                        start=True,
-                        stop=False,
-                    )
-                batch = slice(g * CHUNK + j * P, g * CHUNK + (j + 1) * P)
-                nc.tensor.matmul_mx(
-                    out=accs[j][:],
-                    lhsT=h_codes[:, batch].bitcast(FP8X4),
-                    lhsT_scale=h_scales[:, batch],
-                    rhs=w1_codes[:, weights].bitcast(FP8X4),
-                    rhs_scale=w1_scales[:, weights],
-                    start=False,
-                    stop=(g == GROUPS - 1),
-                )
+            nc.tensor.matmul_mx(
+                out=acc[:, 0:OUT_NODES],
+                lhsT=h_codes_of[c][:, batch].bitcast(FP8X4),
+                lhsT_scale=h_scales_of[c][:, batch],
+                rhs=w1_codes[:, weights].bitcast(FP8X4),
+                rhs_scale=w1_scales[:, weights],
+                start=False,
+                stop=(g == GROUPS - 1),
+            )
 
-        def finish(c, accs):
-            rows_of_out = out[c * CHUNK : (c + 1) * CHUNK, :].rearrange("(p j) o -> p j o", j=PACK)
-            for j in range(PACK):
-                result = result_pool.tile([P, OUT_NODES], F32, name="result")
-                nc.vector.tensor_tensor(out=result[:], in0=accs[j][:], in1=out_bias[:], op=ADD)
-                nc.sync.dma_start(out=rows_of_out[:, j, :], in_=result[:])
+        def finish(c, j, acc):
+            result = result_pool.tile([P, OUT_NODES], F32, name="result")
+            nc.vector.tensor_tensor(
+                out=result[:], in0=acc[:, 0:OUT_NODES], in1=out_bias[:], op=ADD
+            )
+            rows_of_out = out[c * CHUNK : (c + 1) * CHUNK, :].rearrange("(p j) o -> p j o", j=TILES)
+            nc.sync.dma_start(out=rows_of_out[:, j, :], in_=result[:])
 
-        for i in range(AT_ONCE):
-            transpose_operand(i)
-            quantise_operand(i)
-        prepare(AT_ONCE)
+        for i in range(FIRST_PIECES + 1):
+            if i < FIRST_PIECES:
+                transpose_piece(i)
+            if i > 0 and i < 5:
+                quantise_piece(i - 1)
 
-        h_codes_of = {}
-        h_scales_of = {}
-        accs_of = {}
-        for step in range(STEPS + LAG):
-            if step < STEPS:
-                c, g = divmod(step, GROUPS)
-                if g == 0:
-                    h_codes_of[c] = hidden_pool.tile(
-                        [P, GROUPS * CHUNK], U32, align_bytes=64, name="h_codes"
-                    )
-                    h_scales_of[c] = hidden_pool.tile(
-                        [P, GROUPS * CHUNK], U8, align_bytes=64, name="h_scales"
-                    )
-                planes = first_stage(c, g)
-            if step >= LAG:
-                late_c, late_g = divmod(step - LAG, GROUPS)
-                if late_g == 0:
-                    accs_of[late_c] = [
-                        sums.tile([P, OUT_NODES], F32, name="acc%d" % j) for j in range(PACK)
-                    ]
-                second_stage(
-                    late_c, late_g, h_codes_of[late_c], h_scales_of[late_c], accs_of[late_c]
-                )
-                if late_g == GROUPS - 1:
-                    finish(late_c, accs_of[late_c])
-            for i in range(PER_STEP):
-                prepare(AT_ONCE + 1 + PER_STEP * step + i)
-            if step < STEPS:
-                columns = slice(g * CHUNK, (g + 1) * CHUNK)
-                regroup_and_quantise(planes, h_codes_of[c][:, columns], h_scales_of[c][:, columns])
+        prepared = FIRST_PIECES
+        quantised_pieces = 4
+        for step in range(STEPS):
+            c, g = divmod(step, GROUPS)
+            first_stage(step)
+            while quantised_pieces < prepared:
+                quantise_piece(quantised_pieces)
+                quantised_pieces += 1
+            now = min((2 if step == 0 else 3) if c == 0 else (1 if g in (0, 1) else 0), len(pieces) - prepared)
+            late_accs = {}
+            if c > 0:
+                for j in LATE_TILES[g]:
+                    late_accs[j] = sums.tile([P, CHUNK], F32, name="acc")
+                    output_pass(c - 1, j, late_accs[j])
+                    for late_g in range(GROUPS):
+                        hidden_pass(c - 1, j, late_g, late_accs[j])
+            if step > 0:
+                regroup_and_quantise(step - 1, 2)
+            for i in range(prepared, prepared + now):
+                transpose_piece(i)
+            prepared += now
+            for j in late_accs:
+                finish(c - 1, j, late_accs[j])
+
+        last = CHUNKS - 1
+        accs = [sums.tile([P, CHUNK], F32, name="acc") for j in range(2)]
+        accs += [banks.tile([P, CHUNK], F32, name="bank") for j in range(2)]
+        for j in range(TILES):
+            output_pass(last, j, accs[j])
+            for g in range(GROUPS - 1):
+                hidden_pass(last, j, g, accs[j])
+        regroup_and_quantise(STEPS - 1, TILES)
+        for j in range(TILES):
+            hidden_pass(last, j, GROUPS - 1, accs[j])
+            finish(last, j, accs[j])

@@ -41,7 +41,7 @@ def tile_spn_kernel(tc, x, w0, w1, biases, out):
         tc.tile_pool(name="rows", bufs=1) as rows_pool,
         tc.tile_pool(name="quantised", bufs=1) as quantised,
         tc.tile_pool(name="grouped", bufs=4) as grouped_pool,
-        tc.tile_pool(name="planes", bufs=3) as planes_pool,
+        tc.tile_pool(name="planes", bufs=4) as planes_pool,
         tc.tile_pool(name="hidden", bufs=2) as hidden_pool,
         tc.tile_pool(name="result", bufs=4) as result_pool,
         tc.psum_pool(name="banks", bufs=6) as banks,
@@ -151,7 +151,7 @@ def tile_spn_kernel(tc, x, w0, w1, biases, out):
                     )
             grouped = grouped_pool.tile([P, PACK * PIECE], BF16, align_bytes=64, name="grouped")
             grouped_of[i] = grouped
-            copy = nc.vector.tensor_copy if i % VECTOR_EVERY == 0 else nc.scalar.copy
+            copy = nc.vector.tensor_copy if i % 3 == 0 else nc.scalar.copy
             copy(
                 out=grouped[:].bitcast(F32).rearrange("p (r b u) -> p r b u", r=2, u=HALF),
                 in_=bank[:].rearrange("p (r u b) -> p r b u", r=2, u=HALF),
@@ -167,60 +167,106 @@ def tile_spn_kernel(tc, x, w0, w1, biases, out):
         planes_of = {}
         accs_of = {}
 
-        def first_stage(step):
+        def first_stage(step, first, width):
             c, g = divmod(step, GROUPS)
-            planes = planes_pool.tile([P, PACK, CHUNK], BF16, name="planes")
-            planes_of[step] = planes
-            batch = slice(c * CHUNK, (c + 1) * CHUNK)
-            for t in range(PACK):
-                nodes = slice(g * K_PASS + t * P, g * K_PASS + (t + 1) * P)
+            planes = planes_pool.tile([P, PACK, width], BF16, name="planes")
+            planes_of[step, first] = planes
+            batch = slice(c * CHUNK + first, c * CHUNK + first + width)
+            in_bank = CHUNK // width
+            for first_t in range(0, PACK, in_bank):
                 bank = banks.tile([P, CHUNK], F32, name="bank")
-                nc.tensor.matmul_mx(
-                    out=bank[:],
-                    lhsT=w0_codes[:, nodes].bitcast(FP8X4),
-                    lhsT_scale=w0_scales[:, nodes],
-                    rhs=x_codes[:, batch].bitcast(FP8X4),
-                    rhs_scale=x_scales[:, batch],
-                    start=True,
-                    stop=True,
-                )
-                nc.scalar.activation(
-                    out=planes[:, t, :],
-                    in_=bank[:],
-                    func=RELU,
-                    bias=hidden_bias[:, g, t : t + 1],
-                    scale=1.0,
+                for i in range(in_bank):
+                    column = g * K_PASS + (first_t + i) * P
+                    nodes = slice(column, column + P)
+                    nc.tensor.matmul_mx(
+                        out=bank[:, i * width : (i + 1) * width],
+                        lhsT=w0_codes[:, nodes].bitcast(FP8X4),
+                        lhsT_scale=w0_scales[:, nodes],
+                        rhs=x_codes[:, batch].bitcast(FP8X4),
+                        rhs_scale=x_scales[:, batch],
+                        start=True,
+                        stop=True,
+                    )
+                for i in range(in_bank):
+                    t = first_t + i
+                    nc.scalar.activation(
+                        out=planes[:, t, :],
+                        in_=bank[:, i * width : (i + 1) * width],
+                        func=RELU,
+                        bias=hidden_bias[:, g, t : t + 1],
+                        scale=1.0,
+                    )
+
+        h_grouped_of = {}
+
+        def first_stage_on_vector(step, first, width):
+            c, g = divmod(step, GROUPS)
+            tile_banks = []
+            for tile_first in range(first, first + width, P):
+                batch = slice(c * CHUNK + tile_first, c * CHUNK + tile_first + P)
+                bank = banks.tile([P, CHUNK], F32, name="bank")
+                for t in range(PACK):
+                    column = g * K_PASS + t * P
+                    nodes = slice(column, column + P)
+                    nc.tensor.matmul_mx(
+                        out=bank[:, t * P : (t + 1) * P],
+                        lhsT=w0_codes[:, nodes].bitcast(FP8X4),
+                        lhsT_scale=w0_scales[:, nodes],
+                        rhs=x_codes[:, batch].bitcast(FP8X4),
+                        rhs_scale=x_scales[:, batch],
+                        start=True,
+                        stop=True,
+                    )
+                tile_banks.append((tile_first, bank))
+            return tile_banks
+
+        def add_bias_on_vector(step, tile_first, bank):
+            g = step % GROUPS
+            nc.vector.tensor_tensor(
+                out=h_grouped_of[step][:, PACK * tile_first : PACK * (tile_first + P)].rearrange(
+                    "p (b t) -> p b t", t=PACK
+                ),
+                in0=bank[:].rearrange("p (t b) -> p b t", t=PACK),
+                in1=hidden_bias[:, g, :].unsqueeze(1).to_broadcast([P, P, PACK]),
+                op=ADD,
+            )
+
+        def relu_on_vector(step, first, width):
+            h_grouped = h_grouped_of[step][:, PACK * first : PACK * (first + width)]
+            nc.vector.tensor_scalar_max(out=h_grouped, in0=h_grouped, scalar1=0.0)
+
+        def h_grouped_tile(step):
+            if step not in h_grouped_of:
+                h_grouped_of[step] = hidden_pool.tile(
+                    [P, PACK * CHUNK], BF16, align_bytes=64, name="h_grouped"
                 )
 
-        def regroup_and_quantise(step, parts):
+        def regroup(step, unit_first, first, width):
+            h_grouped_tile(step)
+            nc.vector.tensor_copy(
+                out=h_grouped_of[step][:, PACK * first : PACK * (first + width)].rearrange(
+                    "p (c i t) -> p c t i", i=4, t=PACK
+                ),
+                in_=planes_of[step, unit_first][
+                    :, :, first - unit_first : first - unit_first + width
+                ].rearrange("p t (c i) -> p c t i", i=4),
+            )
+
+        def quantise_hidden(step, first, width):
             c, g = divmod(step, GROUPS)
-            if g == 0:
+            if c not in h_codes_of:
                 h_codes_of[c] = hidden_pool.tile(
                     [P, GROUPS * CHUNK], U32, align_bytes=64, name="h_codes"
                 )
                 h_scales_of[c] = hidden_pool.tile(
                     [P, GROUPS * CHUNK], U8, align_bytes=64, name="h_scales"
                 )
-            planes = planes_of.pop(step)
-            h_grouped = hidden_pool.tile([P, PACK * CHUNK], BF16, align_bytes=64, name="h_grouped")
-            width = CHUNK // parts
-            for part in range(parts + 1):
-                if part < parts:
-                    batch = slice(part * width, (part + 1) * width)
-                    nc.vector.tensor_copy(
-                        out=h_grouped[:, PACK * part * width : PACK * (part + 1) * width].rearrange(
-                            "p (c i t) -> p c t i", i=4, t=PACK
-                        ),
-                        in_=planes[:, :, batch].rearrange("p t (c i) -> p c t i", i=4),
-                    )
-                if part > 0:
-                    first = (part - 1) * width
-                    columns = slice(g * CHUNK + first, g * CHUNK + first + width)
-                    nc.vector.quantize_mx(
-                        out=h_codes_of[c][:, columns].bitcast(FP8X4),
-                        scales=h_scales_of[c][:, columns],
-                        in_=h_grouped[:, PACK * first : PACK * (first + width)],
-                    )
+            columns = slice(g * CHUNK + first, g * CHUNK + first + width)
+            nc.vector.quantize_mx(
+                out=h_codes_of[c][:, columns].bitcast(FP8X4),
+                scales=h_scales_of[c][:, columns],
+                in_=h_grouped_of[step][:, PACK * first : PACK * (first + width)],
+            )
 
         def output_pass(c, j, acc):
             batch = slice(c * CHUNK + j * P, c * CHUNK + (j + 1) * P)
@@ -261,30 +307,72 @@ def tile_spn_kernel(tc, x, w0, w1, biases, out):
             if i > 0 and i < 5:
                 quantise_piece(i - 1)
 
+        units = []
+        for step in range(STEPS):
+            for route, width in ((0, 256), (1, 256)) if step == 0 else ((0, CHUNK),):
+                first = 0 if not units or units[-1][0] != step else units[-1][1] + units[-1][2]
+                units.append((step, first, width, route))
+
+        waiting = []
+
+        def quantise_one():
+            if waiting:
+                quantise_hidden(*waiting.pop(0))
+
+        def regroup_unit(step, first, width):
+            part_width = max(width // 2, P)
+            for part_first in range(first, first + width, part_width):
+                regroup(step, first, part_first, part_width)
+                quantise_one()
+                waiting.append((step, part_first, part_width))
+
         prepared = FIRST_PIECES
         quantised_pieces = 4
-        for step in range(STEPS):
+        late_accs = []
+        before = None
+        for k, (step, first, width, on_vector) in enumerate(units):
             c, g = divmod(step, GROUPS)
-            first_stage(step)
-            while quantised_pieces < prepared:
-                quantise_piece(quantised_pieces)
-                quantised_pieces += 1
-            now = min((2 if step == 0 else 3) if c == 0 else (1 if g in (0, 1) else 0), len(pieces) - prepared)
-            late_accs = {}
-            if c > 0:
-                for j in LATE_TILES[g]:
-                    late_accs[j] = sums.tile([P, CHUNK], F32, name="acc")
-                    output_pass(c - 1, j, late_accs[j])
-                    for late_g in range(GROUPS):
-                        hidden_pass(c - 1, j, late_g, late_accs[j])
-            if step > 0:
-                regroup_and_quantise(step - 1, 2)
+            if on_vector:
+                tile_banks = first_stage_on_vector(step, first, width)
+            else:
+                first_stage(step, first, width)
+            now = 0
+            if first == 0:
+                now = min((2 if step == 0 else 3) if c == 0 else (1 if g in (0, 1) else 0), len(pieces) - prepared)
+                if c > 0:
+                    for j in LATE_TILES[g]:
+                        acc = sums.tile([P, CHUNK], F32, name="acc")
+                        late_accs.append((c - 1, j, acc))
+                        output_pass(c - 1, j, acc)
+                        for late_g in range(GROUPS):
+                            hidden_pass(c - 1, j, late_g, acc)
+            if before is not None:
+                regroup_unit(*before)
+            before = None if on_vector else (step, first, width)
+            if on_vector:
+                h_grouped_tile(step)
+                for tile_first, bank in tile_banks:
+                    add_bias_on_vector(step, tile_first, bank)
+                quantise_one()
+                relu_on_vector(step, first, width)
+                waiting.append((step, first, width))
+            if first == 0:
+                while quantised_pieces < prepared:
+                    quantise_piece(quantised_pieces)
+                    quantised_pieces += 1
             for i in range(prepared, prepared + now):
                 transpose_piece(i)
             prepared += now
-            for j in late_accs:
-                finish(c - 1, j, late_accs[j])
+            for late in late_accs:
+                finish(*late)
+            late_accs = []
 
+        if before is not None:
+            step, first, width = before
+            for part in range(first, first + width, P):
+                regroup(step, first, part, P)
+                quantise_one()
+                waiting.append((step, part, P))
         last = CHUNKS - 1
         accs = [sums.tile([P, CHUNK], F32, name="acc") for j in range(2)]
         accs += [banks.tile([P, CHUNK], F32, name="bank") for j in range(2)]
@@ -292,7 +380,8 @@ def tile_spn_kernel(tc, x, w0, w1, biases, out):
             output_pass(last, j, accs[j])
             for g in range(GROUPS - 1):
                 hidden_pass(last, j, g, accs[j])
-        regroup_and_quantise(STEPS - 1, TILES)
+        while waiting:
+            quantise_one()
         for j in range(TILES):
             hidden_pass(last, j, GROUPS - 1, accs[j])
             finish(last, j, accs[j])

@@ -28,7 +28,7 @@ STEPS = CHUNKS * GROUPS
 PIECE = 256
 
 FIRST_PIECES = 6
-LATE_TILES = [(), (0, 1), (2,), (3,)]
+LATE_TILES = [(), (0,), (1, 2), (3,)]
 VECTOR_EVERY = 3
 
 FLOPS = 2 * BATCH * X_DIM * (HIDDEN + OUT_NODES) + 2 * BATCH * HIDDEN * OUT_NODES
@@ -41,7 +41,7 @@ def tile_spn_kernel(tc, x, w0, w1, biases, out):
         tc.tile_pool(name="rows", bufs=1) as rows_pool,
         tc.tile_pool(name="quantised", bufs=1) as quantised,
         tc.tile_pool(name="grouped", bufs=4) as grouped_pool,
-        tc.tile_pool(name="planes", bufs=4) as planes_pool,
+        tc.tile_pool(name="planes", bufs=6) as planes_pool,
         tc.tile_pool(name="hidden", bufs=2) as hidden_pool,
         tc.tile_pool(name="result", bufs=4) as result_pool,
         tc.psum_pool(name="banks", bufs=6) as banks,
@@ -49,10 +49,6 @@ def tile_spn_kernel(tc, x, w0, w1, biases, out):
         tc.manual_schedule(),
     ):
         hidden_bias = const.tile([P, GROUPS, PACK], BF16)
-        nc.scalar.dma_start(
-            out=hidden_bias[:],
-            in_=biases[0:HIDDEN].rearrange("(g p t) -> p g t", p=P, t=PACK),
-        )
         identity = const.tile([P, P], F32)
         make_identity(nc, identity[:])
         warm_up = const.tile([P, 1], F32)
@@ -93,9 +89,13 @@ def tile_spn_kernel(tc, x, w0, w1, biases, out):
         def w0_group(g):
             return two_pieces_of_512_rows(w0, g * K_PASS, "w0_rows%d" % g, w0_codes, w0_scales)
 
-        for halves in zip(x_chunk(0), w0_group(0)):
-            for load in halves:
-                load()
+        x0_loads, w0_loads = x_chunk(0), w0_group(0)
+        for load in (x0_loads[0], w0_loads[0], w0_loads[1], x0_loads[1]):
+            load()
+        nc.sync.dma_start(
+            out=hidden_bias[:],
+            in_=biases[0:HIDDEN].rearrange("(g p t) -> p g t", p=P, t=PACK),
+        )
         for g in range(1, GROUPS):
             for load in w0_group(g):
                 load()
@@ -151,7 +151,7 @@ def tile_spn_kernel(tc, x, w0, w1, biases, out):
                     )
             grouped = grouped_pool.tile([P, PACK * PIECE], BF16, align_bytes=64, name="grouped")
             grouped_of[i] = grouped
-            copy = nc.vector.tensor_copy if i % 3 == 0 else nc.scalar.copy
+            copy = nc.vector.tensor_copy if i % 5 in (0, 3) else nc.scalar.copy
             copy(
                 out=grouped[:].bitcast(F32).rearrange("p (r b u) -> p r b u", r=2, u=HALF),
                 in_=bank[:].rearrange("p (r u b) -> p r b u", r=2, u=HALF),
@@ -309,7 +309,7 @@ def tile_spn_kernel(tc, x, w0, w1, biases, out):
 
         units = []
         for step in range(STEPS):
-            for route, width in ((0, 256), (1, 256)) if step == 0 else ((0, CHUNK),):
+            for route, width in ((0, 256), (1, 256)) if step in (0,) else ((0, 256),) * 2 if step >= 13 else ((0, CHUNK),):
                 first = 0 if not units or units[-1][0] != step else units[-1][1] + units[-1][2]
                 units.append((step, first, width, route))
 
@@ -374,8 +374,9 @@ def tile_spn_kernel(tc, x, w0, w1, biases, out):
                 quantise_one()
                 waiting.append((step, part, P))
         last = CHUNKS - 1
-        accs = [sums.tile([P, CHUNK], F32, name="acc") for j in range(2)]
+        accs = [sums.tile([P, CHUNK], F32, name="acc")]
         accs += [banks.tile([P, CHUNK], F32, name="bank") for j in range(2)]
+        accs += [sums.tile([P, CHUNK], F32, name="acc")]
         for j in range(TILES):
             output_pass(last, j, accs[j])
             for g in range(GROUPS - 1):

@@ -46,7 +46,14 @@ def tile_spn_kernel(tc, x, w0, w1, biases, out):
         tc.tile_pool(name="result", bufs=4) as result_pool,
         tc.psum_pool(name="banks", bufs=6) as banks,
         tc.psum_pool(name="sums", bufs=2) as sums,
-        tc.manual_schedule(),
+        tc.manual_schedule(
+            engines={
+                mybir.EngineType.PE,
+                mybir.EngineType.Activation,
+                mybir.EngineType.Pool,
+                mybir.EngineType.SP,
+            }
+        ),
     ):
         hidden_bias = const.tile([P, GROUPS, PACK], BF16)
         identity = const.tile([P, P], F32)

@@ -28,7 +28,8 @@ STEPS = CHUNKS * GROUPS
 PIECE = 256
 
 FIRST_PIECES = 6
-LATE_TILES = [(), (0,), (1, 2), (3,)]
+LATE_STEPS = (2, 3, 4, 5)
+LATE_STEPS_AT_END = (2, 3, 3, 4)
 VECTOR_EVERY = 3
 
 FLOPS = 2 * BATCH * X_DIM * (HIDDEN + OUT_NODES) + 2 * BATCH * HIDDEN * OUT_NODES
@@ -320,6 +321,12 @@ def tile_spn_kernel(tc, x, w0, w1, biases, out):
                 first = 0 if not units or units[-1][0] != step else units[-1][1] + units[-1][2]
                 units.append((step, first, width, route))
 
+        tiles_due = {step: [] for step in range(STEPS)}
+        for late_c in range(CHUNKS - 1):
+            for j in range(TILES):
+                late_steps = LATE_STEPS if late_c < CHUNKS - 2 else LATE_STEPS_AT_END
+                tiles_due[late_c * GROUPS + GROUPS - 1 + late_steps[j]].append((late_c, j))
+
         waiting = []
 
         def quantise_one():
@@ -345,14 +352,13 @@ def tile_spn_kernel(tc, x, w0, w1, biases, out):
                 first_stage(step, first, width)
             now = 0
             if first == 0:
-                now = min((2 if step == 0 else 3) if c == 0 else (1 if g in (0, 1) else 0), len(pieces) - prepared)
-                if c > 0:
-                    for j in LATE_TILES[g]:
-                        acc = sums.tile([P, CHUNK], F32, name="acc")
-                        late_accs.append((c - 1, j, acc))
-                        output_pass(c - 1, j, acc)
-                        for late_g in range(GROUPS):
-                            hidden_pass(c - 1, j, late_g, acc)
+                now = min((2 if step == 0 else 3) if c == 0 else (2 if g == 0 else 0), len(pieces) - prepared)
+                for late_c, j in tiles_due[step]:
+                    acc = sums.tile([P, CHUNK], F32, name="acc")
+                    late_accs.append((late_c, j, acc))
+                    output_pass(late_c, j, acc)
+                    for late_g in range(GROUPS):
+                        hidden_pass(late_c, j, late_g, acc)
             if before is not None:
                 regroup_unit(*before)
             before = None if on_vector else (step, first, width)

@@ -27,10 +27,11 @@ STEPS = CHUNKS * GROUPS
 
 PIECE = 256
 
-FIRST_PIECES = 6
-LATE_STEPS = (2, 3, 4, 5)
-LATE_STEPS_AT_END = (2, 3, 3, 4)
-VECTOR_EVERY = 3
+FIRST_PIECES = 5
+SPLIT_PIECES = 6
+FIRST_LATE_STEP = 1
+HALVED_STEPS = range(STEPS - 3, STEPS)
+
 
 FLOPS = 2 * BATCH * X_DIM * (HIDDEN + OUT_NODES) + 2 * BATCH * HIDDEN * OUT_NODES
 
@@ -84,7 +85,12 @@ def tile_spn_kernel(tc, x, w0, w1, biases, out):
 
                 def load(j=j, columns=columns):
                     rows = rows_pool.tile([P, 2, X_DIM], BF16, name="%s_%d" % (name, j))
-                    nc.sync.dma_start(out=rows[:], in_=by_partition[:, j : j + 2, :])
+                    rows_a_load = 2 if pieces else 1
+                    for r in range(0, 2, rows_a_load):
+                        nc.sync.dma_start(
+                            out=rows[:, r : r + rows_a_load, :],
+                            in_=by_partition[:, j + r : j + r + rows_a_load, :],
+                        )
                     row_tiles = [row_tile(rows[:, r, :], 0) for r in range(2)]
                     pieces.append((row_tiles, codes[:, columns], scales[:, columns]))
 
@@ -148,22 +154,28 @@ def tile_spn_kernel(tc, x, w0, w1, biases, out):
         grouped_of = {}
 
         def transpose_piece(i):
-            bank = banks.tile([P, CHUNK], F32, name="bank")
-            for r in range(2):
-                for u in range(HALF):
-                    quarter = HALF * r + u
-                    nc.tensor.transpose(
-                        bank[:, P * quarter : P * (quarter + 1)],
-                        pieces[i][0][r][u],
-                        identity[:],
-                    )
             grouped = grouped_pool.tile([P, PACK * PIECE], BF16, align_bytes=64, name="grouped")
             grouped_of[i] = grouped
-            copy = nc.vector.tensor_copy if i % 5 in (0, 3) else nc.scalar.copy
-            copy(
-                out=grouped[:].bitcast(F32).rearrange("p (r b u) -> p r b u", r=2, u=HALF),
-                in_=bank[:].rearrange("p (r u b) -> p r b u", r=2, u=HALF),
-            )
+            words = grouped[:].bitcast(F32).rearrange("p (r b u) -> p r b u", r=2, u=HALF)
+            tiles_a_bank = 1 if i < SPLIT_PIECES else 2
+            for first_r in range(0, 2, tiles_a_bank):
+                bank = banks.tile([P, CHUNK], F32, name="bank")
+                for r in range(tiles_a_bank):
+                    for u in range(HALF):
+                        quarter = HALF * r + u
+                        nc.tensor.transpose(
+                            bank[:, P * quarter : P * (quarter + 1)],
+                            pieces[i][0][first_r + r][u],
+                            identity[:],
+                        )
+                on_vector = first_r == 0 if tiles_a_bank == 1 else i % 5 in (0, 3)
+                copy = nc.vector.tensor_copy if on_vector else nc.scalar.copy
+                copy(
+                    out=words[:, first_r : first_r + tiles_a_bank],
+                    in_=bank[:, 0 : HALF * P * tiles_a_bank].rearrange(
+                        "p (r u b) -> p r b u", r=tiles_a_bank, u=HALF
+                    ),
+                )
 
         def quantise_piece(i):
             nc.vector.quantize_mx(
@@ -249,9 +261,10 @@ def tile_spn_kernel(tc, x, w0, w1, biases, out):
                     [P, PACK * CHUNK], BF16, align_bytes=64, name="h_grouped"
                 )
 
-        def regroup(step, unit_first, first, width):
+        def regroup(step, unit_first, first, width, on_scalar=False):
             h_grouped_tile(step)
-            nc.vector.tensor_copy(
+            copy = nc.scalar.copy if on_scalar else nc.vector.tensor_copy
+            copy(
                 out=h_grouped_of[step][:, PACK * first : PACK * (first + width)].rearrange(
                     "p (c i t) -> p c t i", i=4, t=PACK
                 ),
@@ -309,23 +322,37 @@ def tile_spn_kernel(tc, x, w0, w1, biases, out):
             rows_of_out = out[c * CHUNK : (c + 1) * CHUNK, :].rearrange("(p j) o -> p j o", j=TILES)
             nc.sync.dma_start(out=rows_of_out[:, j, :], in_=result[:])
 
-        for i in range(FIRST_PIECES + 1):
-            if i < FIRST_PIECES:
-                transpose_piece(i)
-            if i > 0 and i < 5:
-                quantise_piece(i - 1)
+        to_transpose = list(range(len(pieces)))
+        to_quantise = list(range(len(pieces)))
+
+        def transpose_pieces(n):
+            for i in range(min(n, len(to_transpose))):
+                transpose_piece(to_transpose.pop(0))
+
+        def quantise_pieces(n):
+            for i in range(n):
+                quantise_piece(to_quantise.pop(0))
+
+        for i in range(FIRST_PIECES):
+            transpose_pieces(1)
+            if i in (1, 2, 3):
+                quantise_pieces(1)
 
         units = []
         for step in range(STEPS):
-            for route, width in ((0, 256), (1, 256)) if step in (0,) else ((0, 256),) * 2 if step >= 13 else ((0, CHUNK),):
+            for route, width in ((0, 256), (1, 256)) if step in (0,) else ((0, 256),) * 2 if step in HALVED_STEPS else ((0, CHUNK),):
                 first = 0 if not units or units[-1][0] != step else units[-1][1] + units[-1][2]
                 units.append((step, first, width, route))
 
-        tiles_due = {step: [] for step in range(STEPS)}
+        tiles_due = {}
         for late_c in range(CHUNKS - 1):
             for j in range(TILES):
-                late_steps = LATE_STEPS if late_c < CHUNKS - 2 else LATE_STEPS_AT_END
-                tiles_due[late_c * GROUPS + GROUPS - 1 + late_steps[j]].append((late_c, j))
+                step = (late_c + 1) * GROUPS + FIRST_LATE_STEP + j
+                first = 0
+                if late_c == CHUNKS - 2:
+                    step, half = divmod(2 * ((late_c + 1) * GROUPS + FIRST_LATE_STEP) + j, 2)
+                    first = half * CHUNK // 2
+                tiles_due[step, first] = (late_c, j)
 
         waiting = []
 
@@ -340,8 +367,6 @@ def tile_spn_kernel(tc, x, w0, w1, biases, out):
                 quantise_one()
                 waiting.append((step, part_first, part_width))
 
-        prepared = FIRST_PIECES
-        quantised_pieces = 4
         late_accs = []
         before = None
         for k, (step, first, width, on_vector) in enumerate(units):
@@ -350,15 +375,13 @@ def tile_spn_kernel(tc, x, w0, w1, biases, out):
                 tile_banks = first_stage_on_vector(step, first, width)
             else:
                 first_stage(step, first, width)
-            now = 0
-            if first == 0:
-                now = min((2 if step == 0 else 3) if c == 0 else (2 if g == 0 else 0), len(pieces) - prepared)
-                for late_c, j in tiles_due[step]:
-                    acc = sums.tile([P, CHUNK], F32, name="acc")
-                    late_accs.append((late_c, j, acc))
-                    output_pass(late_c, j, acc)
-                    for late_g in range(GROUPS):
-                        hidden_pass(late_c, j, late_g, acc)
+            if (step, first) in tiles_due:
+                late_c, j = tiles_due[step, first]
+                acc = sums.tile([P, CHUNK], F32, name="acc")
+                late_accs.append((late_c, j, acc))
+                output_pass(late_c, j, acc)
+                for late_g in range(GROUPS):
+                    hidden_pass(late_c, j, late_g, acc)
             if before is not None:
                 regroup_unit(*before)
             before = None if on_vector else (step, first, width)
@@ -369,23 +392,23 @@ def tile_spn_kernel(tc, x, w0, w1, biases, out):
                 quantise_one()
                 relu_on_vector(step, first, width)
                 waiting.append((step, first, width))
-            if first == 0:
-                while quantised_pieces < prepared:
-                    quantise_piece(quantised_pieces)
-                    quantised_pieces += 1
-            for i in range(prepared, prepared + now):
-                transpose_piece(i)
-            prepared += now
+            if first == 0 and step == 0:
+                quantise_pieces(1)
+                transpose_pieces(1)
+                quantise_pieces(2)
+                transpose_pieces(2)
+            elif first == 0:
+                quantise_pieces(len(to_quantise) - len(to_transpose))
+                transpose_pieces(3 if c == 0 else (2 if g == 0 else 0))
             for late in late_accs:
                 finish(*late)
             late_accs = []
 
-        if before is not None:
-            step, first, width = before
-            for part in range(first, first + width, P):
-                regroup(step, first, part, P)
-                quantise_one()
-                waiting.append((step, part, P))
+        step, first, width = before
+        for part in range(first, first + width, P):
+            regroup(step, first, part, P, on_scalar=part + P == CHUNK)
+            quantise_one()
+            waiting.append((step, part, P))
         last = CHUNKS - 1
         accs = [sums.tile([P, CHUNK], F32, name="acc")]
         accs += [banks.tile([P, CHUNK], F32, name="bank") for j in range(2)]

@@ -46,8 +46,7 @@ def tile_spn_kernel(tc, x, w0, w1, biases, out):
         tc.tile_pool(name="planes", bufs=6) as planes_pool,
         tc.tile_pool(name="hidden", bufs=2) as hidden_pool,
         tc.tile_pool(name="result", bufs=4) as result_pool,
-        tc.psum_pool(name="banks", bufs=6) as banks,
-        tc.psum_pool(name="sums", bufs=2) as sums,
+        tc.psum_pool(name="banks", bufs=8) as banks,
         tc.manual_schedule(
             engines={
                 mybir.EngineType.PE,
@@ -261,7 +260,7 @@ def tile_spn_kernel(tc, x, w0, w1, biases, out):
                     [P, PACK * CHUNK], BF16, align_bytes=64, name="h_grouped"
                 )
 
-        def regroup(step, unit_first, first, width, on_scalar=False):
+        def regroup(step, unit_first, first, width, on_scalar):
             h_grouped_tile(step)
             copy = nc.scalar.copy if on_scalar else nc.vector.tensor_copy
             copy(
@@ -363,7 +362,8 @@ def tile_spn_kernel(tc, x, w0, w1, biases, out):
         def regroup_unit(step, first, width):
             part_width = max(width // 2, P)
             for part_first in range(first, first + width, part_width):
-                regroup(step, first, part_first, part_width)
+                on_scalar = step == STEPS - 1 and part_first > first
+                regroup(step, first, part_first, part_width, on_scalar)
                 quantise_one()
                 waiting.append((step, part_first, part_width))
 
@@ -377,7 +377,7 @@ def tile_spn_kernel(tc, x, w0, w1, biases, out):
                 first_stage(step, first, width)
             if (step, first) in tiles_due:
                 late_c, j = tiles_due[step, first]
-                acc = sums.tile([P, CHUNK], F32, name="acc")
+                acc = banks.tile([P, CHUNK], F32, name="bank")
                 late_accs.append((late_c, j, acc))
                 output_pass(late_c, j, acc)
                 for late_g in range(GROUPS):
@@ -404,15 +404,9 @@ def tile_spn_kernel(tc, x, w0, w1, biases, out):
                 finish(*late)
             late_accs = []
 
-        step, first, width = before
-        for part in range(first, first + width, P):
-            regroup(step, first, part, P, on_scalar=part + P == CHUNK)
-            quantise_one()
-            waiting.append((step, part, P))
+        regroup_unit(*before)
         last = CHUNKS - 1
-        accs = [sums.tile([P, CHUNK], F32, name="acc")]
-        accs += [banks.tile([P, CHUNK], F32, name="bank") for j in range(2)]
-        accs += [sums.tile([P, CHUNK], F32, name="acc")]
+        accs = [banks.tile([P, CHUNK], F32, name="bank") for j in range(TILES)]
         for j in range(TILES):
             output_pass(last, j, accs[j])
             for g in range(GROUPS - 1):

@@ -30,7 +30,7 @@ PIECE = 256
 FIRST_PIECES = 5
 SPLIT_PIECES = 6
 FIRST_LATE_STEP = 1
-HALVED_STEPS = range(STEPS - 3, STEPS)
+HALVED_STEPS = range(STEPS - 2, STEPS)
 
 
 FLOPS = 2 * BATCH * X_DIM * (HIDDEN + OUT_NODES) + 2 * BATCH * HIDDEN * OUT_NODES
@@ -346,12 +346,9 @@ def tile_spn_kernel(tc, x, w0, w1, biases, out):
         tiles_due = {}
         for late_c in range(CHUNKS - 1):
             for j in range(TILES):
-                step = (late_c + 1) * GROUPS + FIRST_LATE_STEP + j
-                first = 0
-                if late_c == CHUNKS - 2:
-                    step, half = divmod(2 * ((late_c + 1) * GROUPS + FIRST_LATE_STEP) + j, 2)
-                    first = half * CHUNK // 2
-                tiles_due[step, first] = (late_c, j)
+                a_step = 2 if late_c == CHUNKS - 2 else 1
+                step = (late_c + 1) * GROUPS + FIRST_LATE_STEP + j // a_step
+                tiles_due.setdefault(step, []).append((late_c, j))
 
         waiting = []
 
@@ -375,8 +372,7 @@ def tile_spn_kernel(tc, x, w0, w1, biases, out):
                 tile_banks = first_stage_on_vector(step, first, width)
             else:
                 first_stage(step, first, width)
-            if (step, first) in tiles_due:
-                late_c, j = tiles_due[step, first]
+            for late_c, j in tiles_due.get(step, ()) if first == 0 else ():
                 acc = banks.tile([P, CHUNK], F32, name="bank")
                 late_accs.append((late_c, j, acc))
                 output_pass(late_c, j, acc)

import concourse.mybir as mybir
from concourse.masks import make_identity

BF16 = mybir.dt.bfloat16
F32 = mybir.dt.float32
U32 = mybir.dt.uint32
U8 = mybir.dt.uint8
FP8X4 = mybir.dt.float8_e4m3fn_x4
RELU = mybir.ActivationFunctionType.Relu
ADD = mybir.AluOpType.add

P = 128
PACK = 4
K_PASS = P * PACK
HALF = 2

BATCH = 2048
X_DIM = 512
HIDDEN = 2048
OUT_NODES = 256

CHUNK = 512
CHUNKS = BATCH // CHUNK
TILES = CHUNK // P
GROUPS = HIDDEN // K_PASS
STEPS = CHUNKS * GROUPS

PIECE = 256

FIRST_PIECES = 5
SPLIT_PIECES = 6
FIRST_LATE_STEP = 1
HALVED_STEPS = range(STEPS - 2, STEPS)


FLOPS = 2 * BATCH * X_DIM * (HIDDEN + OUT_NODES) + 2 * BATCH * HIDDEN * OUT_NODES


def tile_spn_kernel(tc, x, w0, w1, biases, out):
    nc = tc.nc
    with (
        tc.tile_pool(name="const", bufs=1) as const,
        tc.tile_pool(name="rows", bufs=1) as rows_pool,
        tc.tile_pool(name="quantised", bufs=1) as quantised,
        tc.tile_pool(name="grouped", bufs=4) as grouped_pool,
        tc.tile_pool(name="planes", bufs=6) as planes_pool,
        tc.tile_pool(name="hidden", bufs=2) as hidden_pool,
        tc.tile_pool(name="result", bufs=4) as result_pool,
        tc.psum_pool(name="banks", bufs=8) as banks,
        tc.manual_schedule(
            engines={
                mybir.EngineType.PE,
                mybir.EngineType.Activation,
                mybir.EngineType.Pool,
                mybir.EngineType.SP,
            }
        ),
    ):
        hidden_bias = const.tile([P, GROUPS, PACK], BF16)
        identity = const.tile([P, P], F32)
        make_identity(nc, identity[:])
        warm_up = const.tile([P, 1], F32)
        nc.vector.memset(warm_up[:], 0.0)
        nc.scalar.activation(out=warm_up[:], in_=warm_up[:], func=RELU)

        x_codes = quantised.tile([P, BATCH], U32, align_bytes=64)
        x_scales = quantised.tile([P, BATCH], U8, align_bytes=64)
        w0_codes = quantised.tile([P, HIDDEN + OUT_NODES], U32, align_bytes=64)
        w0_scales = quantised.tile([P, HIDDEN + OUT_NODES], U8, align_bytes=64)
        w1_codes = quantised.tile([P, GROUPS * OUT_NODES], U32, align_bytes=64)
        w1_scales = quantised.tile([P, GROUPS * OUT_NODES], U8, align_bytes=64)

        pieces = []

        def row_tile(rows, g):
            words = rows.bitcast(F32)
            return [words[:, HALF * P * g + u : HALF * P * (g + 1) : HALF] for u in range(HALF)]

        def two_pieces_of_512_rows(source, first, name, codes, scales):
            by_partition = source[first : first + K_PASS, :].rearrange("(p j) k -> p j k", j=PACK)
            halves = []
            for j in range(0, PACK, 2):
                columns = slice(first + P * j, first + P * j + PIECE)

                def load(j=j, columns=columns):
                    rows = rows_pool.tile([P, 2, X_DIM], BF16, name="%s_%d" % (name, j))
                    rows_a_load = 2 if pieces else 1
                    for r in range(0, 2, rows_a_load):
                        nc.sync.dma_start(
                            out=rows[:, r : r + rows_a_load, :],
                            in_=by_partition[:, j + r : j + r + rows_a_load, :],
                        )
                    row_tiles = [row_tile(rows[:, r, :], 0) for r in range(2)]
                    pieces.append((row_tiles, codes[:, columns], scales[:, columns]))

                halves.append(load)
            return halves

        def x_chunk(c):
            return two_pieces_of_512_rows(x, c * CHUNK, "x_rows%d" % c, x_codes, x_scales)

        def w0_group(g):
            return two_pieces_of_512_rows(w0, g * K_PASS, "w0_rows%d" % g, w0_codes, w0_scales)

        x0_loads, w0_loads = x_chunk(0), w0_group(0)
        for load in (x0_loads[0], w0_loads[0], w0_loads[1], x0_loads[1]):
            load()
        nc.sync.dma_start(
            out=hidden_bias[:],
            in_=biases[0:HIDDEN].rearrange("(g p t) -> p g t", p=P, t=PACK),
        )
        for g in range(1, GROUPS):
            for load in w0_group(g):
                load()
        for load in x_chunk(1):
            load()

        w0_out_rows = rows_pool.tile([P, OUT_NODES // P, X_DIM], BF16)
        nc.sync.dma_start(
            out=w0_out_rows[:],
            in_=w0[HIDDEN : HIDDEN + OUT_NODES, :].rearrange("(a p) k -> p a k", p=P),
        )
        out_columns = slice(HIDDEN, HIDDEN + OUT_NODES)
        pieces.append(
            (
                [row_tile(w0_out_rows[:, a, :], 0) for a in range(OUT_NODES // P)],
                w0_codes[:, out_columns],
                w0_scales[:, out_columns],
            )
        )
        w1_rows = rows_pool.tile([P, OUT_NODES // P, HIDDEN], BF16)
        nc.sync.dma_start(out=w1_rows[:], in_=w1.rearrange("(a p) k -> p a k", p=P))
        for g in range(GROUPS):
            columns = slice(g * OUT_NODES, (g + 1) * OUT_NODES)
            pieces.append(
                (
                    [row_tile(w1_rows[:, a, :], g) for a in range(OUT_NODES // P)],
                    w1_codes[:, columns],
                    w1_scales[:, columns],
                )
            )
        for c in range(2, CHUNKS):
            for load in x_chunk(c):
                load()

        out_bias_bf = const.tile([P, OUT_NODES], BF16)
        nc.sync.dma_start(
            out=out_bias_bf[:], in_=biases[HIDDEN : HIDDEN + OUT_NODES].partition_broadcast(P)
        )
        out_bias = const.tile([P, OUT_NODES], F32)
        nc.gpsimd.tensor_copy(out=out_bias[:], in_=out_bias_bf[:])

        grouped_of = {}

        def transpose_piece(i):
            grouped = grouped_pool.tile([P, PACK * PIECE], BF16, align_bytes=64, name="grouped")
            grouped_of[i] = grouped
            words = grouped[:].bitcast(F32).rearrange("p (r b u) -> p r b u", r=2, u=HALF)
            tiles_a_bank = 1 if i < SPLIT_PIECES else 2
            for first_r in range(0, 2, tiles_a_bank):
                bank = banks.tile([P, CHUNK], F32, name="bank")
                for r in range(tiles_a_bank):
                    for u in range(HALF):
                        quarter = HALF * r + u
                        nc.tensor.transpose(
                            bank[:, P * quarter : P * (quarter + 1)],
                            pieces[i][0][first_r + r][u],
                            identity[:],
                        )
                on_vector = first_r == 0 if tiles_a_bank == 1 else i % 5 in (0, 3)
                copy = nc.vector.tensor_copy if on_vector else nc.scalar.copy
                copy(
                    out=words[:, first_r : first_r + tiles_a_bank],
                    in_=bank[:, 0 : HALF * P * tiles_a_bank].rearrange(
                        "p (r u b) -> p r b u", r=tiles_a_bank, u=HALF
                    ),
                )

        def quantise_piece(i):
            nc.vector.quantize_mx(
                out=pieces[i][1].bitcast(FP8X4), scales=pieces[i][2], in_=grouped_of[i][:]
            )

        h_codes_of = {}
        h_scales_of = {}
        planes_of = {}
        accs_of = {}

        def first_stage(step, first, width):
            c, g = divmod(step, GROUPS)
            planes = planes_pool.tile([P, PACK, width], BF16, name="planes")
            planes_of[step, first] = planes
            batch = slice(c * CHUNK + first, c * CHUNK + first + width)
            in_bank = CHUNK // width
            for first_t in range(0, PACK, in_bank):
                bank = banks.tile([P, CHUNK], F32, name="bank")
                for i in range(in_bank):
                    column = g * K_PASS + (first_t + i) * P
                    nodes = slice(column, column + P)
                    nc.tensor.matmul_mx(
                        out=bank[:, i * width : (i + 1) * width],
                        lhsT=w0_codes[:, nodes].bitcast(FP8X4),
                        lhsT_scale=w0_scales[:, nodes],
                        rhs=x_codes[:, batch].bitcast(FP8X4),
                        rhs_scale=x_scales[:, batch],
                        start=True,
                        stop=True,
                    )
                for i in range(in_bank):
                    t = first_t + i
                    nc.scalar.activation(
                        out=planes[:, t, :],
                        in_=bank[:, i * width : (i + 1) * width],
                        func=RELU,
                        bias=hidden_bias[:, g, t : t + 1],
                        scale=1.0,
                    )

        h_grouped_of = {}

        def first_stage_on_vector(step, first, width):
            c, g = divmod(step, GROUPS)
            tile_banks = []
            for tile_first in range(first, first + width, P):
                batch = slice(c * CHUNK + tile_first, c * CHUNK + tile_first + P)
                bank = banks.tile([P, CHUNK], F32, name="bank")
                for t in range(PACK):
                    column = g * K_PASS + t * P
                    nodes = slice(column, column + P)
                    nc.tensor.matmul_mx(
                        out=bank[:, t * P : (t + 1) * P],
                        lhsT=w0_codes[:, nodes].bitcast(FP8X4),
                        lhsT_scale=w0_scales[:, nodes],
                        rhs=x_codes[:, batch].bitcast(FP8X4),
                        rhs_scale=x_scales[:, batch],
                        start=True,
                        stop=True,
                    )
                tile_banks.append((tile_first, bank))
            return tile_banks

        def add_bias_on_vector(step, tile_first, bank):
            g = step % GROUPS
            nc.vector.tensor_tensor(
                out=h_grouped_of[step][:, PACK * tile_first : PACK * (tile_first + P)].rearrange(
                    "p (b t) -> p b t", t=PACK
                ),
                in0=bank[:].rearrange("p (t b) -> p b t", t=PACK),
                in1=hidden_bias[:, g, :].unsqueeze(1).to_broadcast([P, P, PACK]),
                op=ADD,
            )

        def relu_on_vector(step, first, width):
            h_grouped = h_grouped_of[step][:, PACK * first : PACK * (first + width)]
            nc.vector.tensor_scalar_max(out=h_grouped, in0=h_grouped, scalar1=0.0)

        def h_grouped_tile(step):
            if step not in h_grouped_of:
                h_grouped_of[step] = hidden_pool.tile(
                    [P, PACK * CHUNK], BF16, align_bytes=64, name="h_grouped"
                )

        def regroup(step, unit_first, first, width, on_scalar):
            h_grouped_tile(step)
            copy = nc.scalar.copy if on_scalar else nc.vector.tensor_copy
            copy(
                out=h_grouped_of[step][:, PACK * first : PACK * (first + width)].rearrange(
                    "p (c i t) -> p c t i", i=4, t=PACK
                ),
                in_=planes_of[step, unit_first][
                    :, :, first - unit_first : first - unit_first + width
                ].rearrange("p t (c i) -> p c t i", i=4),
            )

        def quantise_hidden(step, first, width):
            c, g = divmod(step, GROUPS)
            if c not in h_codes_of:
                h_codes_of[c] = hidden_pool.tile(
                    [P, GROUPS * CHUNK], U32, align_bytes=64, name="h_codes"
                )
                h_scales_of[c] = hidden_pool.tile(
                    [P, GROUPS * CHUNK], U8, align_bytes=64, name="h_scales"
                )
            columns = slice(g * CHUNK + first, g * CHUNK + first + width)
            nc.vector.quantize_mx(
                out=h_codes_of[c][:, columns].bitcast(FP8X4),
                scales=h_scales_of[c][:, columns],
                in_=h_grouped_of[step][:, PACK * first : PACK * (first + width)],
            )

        def output_pass(c, j, acc):
            batch = slice(c * CHUNK + j * P, c * CHUNK + (j + 1) * P)
            nc.tensor.matmul_mx(
                out=acc[:, 0:OUT_NODES],
                lhsT=x_codes[:, batch].bitcast(FP8X4),
                lhsT_scale=x_scales[:, batch],
                rhs=w0_codes[:, out_columns].bitcast(FP8X4),
                rhs_scale=w0_scales[:, out_columns],
                start=True,
                stop=False,
            )

        def hidden_pass(c, j, g, acc):
            batch = slice(g * CHUNK + j * P, g * CHUNK + (j + 1) * P)
            weights = slice(g * OUT_NODES, (g + 1) * OUT_NODES)
            nc.tensor.matmul_mx(
                out=acc[:, 0:OUT_NODES],
                lhsT=h_codes_of[c][:, batch].bitcast(FP8X4),
                lhsT_scale=h_scales_of[c][:, batch],
                rhs=w1_codes[:, weights].bitcast(FP8X4),
                rhs_scale=w1_scales[:, weights],
                start=False,
                stop=(g == GROUPS - 1),
            )

        def finish(c, j, acc):
            result = result_pool.tile([P, OUT_NODES], F32, name="result")
            nc.vector.tensor_tensor(
                out=result[:], in0=acc[:, 0:OUT_NODES], in1=out_bias[:], op=ADD
            )
            rows_of_out = out[c * CHUNK : (c + 1) * CHUNK, :].rearrange("(p j) o -> p j o", j=TILES)
            nc.sync.dma_start(out=rows_of_out[:, j, :], in_=result[:])

        to_transpose = list(range(len(pieces)))
        to_quantise = list(range(len(pieces)))

        def transpose_pieces(n):
            for i in range(min(n, len(to_transpose))):
                transpose_piece(to_transpose.pop(0))

        def quantise_pieces(n):
            for i in range(n):
                quantise_piece(to_quantise.pop(0))

        for i in range(FIRST_PIECES):
            transpose_pieces(1)
            if i in (1, 2, 3):
                quantise_pieces(1)

        units = []
        for step in range(STEPS):
            for route, width in ((0, 256), (1, 256)) if step in (0,) else ((0, 256),) * 2 if step in HALVED_STEPS else ((0, CHUNK),):
                first = 0 if not units or units[-1][0] != step else units[-1][1] + units[-1][2]
                units.append((step, first, width, route))

        tiles_due = {}
        for late_c in range(CHUNKS - 1):
            for j in range(TILES):
                a_step = 2 if late_c == CHUNKS - 2 else 1
                step = (late_c + 1) * GROUPS + FIRST_LATE_STEP + j // a_step
                tiles_due.setdefault(step, []).append((late_c, j))

        waiting = []

        def quantise_one():
            if waiting:
                quantise_hidden(*waiting.pop(0))

        def regroup_unit(step, first, width):
            part_width = max(width // 2, P)
            for part_first in range(first, first + width, part_width):
                on_scalar = step == STEPS - 1 and part_first > first
                regroup(step, first, part_first, part_width, on_scalar)
                quantise_one()
                waiting.append((step, part_first, part_width))

        late_accs = []
        before = None
        for k, (step, first, width, on_vector) in enumerate(units):
            c, g = divmod(step, GROUPS)
            if on_vector:
                tile_banks = first_stage_on_vector(step, first, width)
            else:
                first_stage(step, first, width)
            for late_c, j in tiles_due.get(step, ()) if first == 0 else ():
                acc = banks.tile([P, CHUNK], F32, name="bank")
                late_accs.append((late_c, j, acc))
                output_pass(late_c, j, acc)
                for late_g in range(GROUPS):
                    hidden_pass(late_c, j, late_g, acc)
            if before is not None:
                regroup_unit(*before)
            before = None if on_vector else (step, first, width)
            if on_vector:
                h_grouped_tile(step)
                for tile_first, bank in tile_banks:
                    add_bias_on_vector(step, tile_first, bank)
                quantise_one()
                relu_on_vector(step, first, width)
                waiting.append((step, first, width))
            if first == 0 and step == 0:
                quantise_pieces(1)
                transpose_pieces(1)
                quantise_pieces(2)
                transpose_pieces(2)
            elif first == 0:
                quantise_pieces(len(to_quantise) - len(to_transpose))
                transpose_pieces(3 if c == 0 else (2 if g == 0 else 0))
            for late in late_accs:
                finish(*late)
            late_accs = []

        regroup_unit(*before)
        last = CHUNKS - 1
        accs = [banks.tile([P, CHUNK], F32, name="bank") for j in range(TILES)]
        for j in range(TILES):
            output_pass(last, j, accs[j])
            for g in range(GROUPS - 1):
                hidden_pass(last, j, g, accs[j])
        while waiting:
            quantise_one()
        for j in range(TILES):
            hidden_pass(last, j, GROUPS - 1, accs[j])
            finish(last, j, accs[j])
